import numpy as np
import ml_dtypes


def mxq(x, axis, fmt="e4m3"):
    dtype, down = {"e4m3": (ml_dtypes.float8_e4m3fn, 7), "e5m2": (ml_dtypes.float8_e5m2, 14)}[fmt]
    v = np.moveaxis(np.asarray(x, np.float32).astype(ml_dtypes.bfloat16).astype(np.float64), axis, -1)
    blocks = v.reshape(v.shape[:-1] + (-1, 32))
    amax = np.abs(blocks).max(-1, keepdims=True)
    byte = np.maximum(np.where(amax > 0, np.frexp(amax)[1] - 1 + 127, 0) - down, 1)
    scale = np.exp2(byte - 127.0)
    codes = (blocks / scale).astype(np.float32).astype(dtype).astype(np.float64)
    return np.moveaxis((codes * scale).reshape(v.shape), -1, axis)


WIDE = False


def mx_kscale(k):
    if not WIDE:
        return np.ones(k)
    levels = np.array([10, -10, 5, -5, 0])
    if k % 512:
        return np.exp2(np.random.permutation(np.resize(levels, k // 32))).repeat(32)
    a = np.empty((k // 512, 16))
    for p in range(k // 512):
        a[p, :8] = np.random.permutation(np.resize(levels, 8))
        for g in range(8):
            far = levels[np.abs(levels - a[p, g]) >= 10]
            a[p, g + 8] = far[np.random.randint(len(far))]
    return np.exp2(a.ravel()).repeat(32)


BF16 = ml_dtypes.bfloat16


def bf(x):
    return np.asarray(x, np.float32).astype(BF16)


def f64(x):
    return np.asarray(x).astype(np.float64)


E2M1 = np.array([0.0, 0.5, 1.0, 1.5, 2.0, 3.0, 4.0, 6.0, -0.0, -0.5, -1.0, -1.5, -2.0, -3.0, -4.0, -6.0])


def pack_weight(w, fmt):
    k, n = w.shape
    w = f64(bf(w)).reshape(k // 32, 32, n)
    amax = np.abs(w).max(1)
    if fmt == "e4m3":
        byte = np.frexp(amax)[1] - 1 + 127 - 7
    else:
        mant, ex = np.frexp(amax / 6.0)
        byte = np.where(mant > 0.5, ex, ex - 1) + 127
    byte = np.clip(np.where(amax > 0, byte, 1), 1, 254)
    scaled = (w * np.exp2(127.0 - byte)[:, None, :]).reshape(k, n).astype(np.float32)
    by_word = np.ascontiguousarray(scaled.reshape(k // 512, 128, 4, n).transpose(0, 1, 3, 2))
    if fmt == "e4m3":
        words = by_word.astype(ml_dtypes.float8_e4m3fn).view(np.uint8)
    else:
        c = by_word.astype(ml_dtypes.float4_e2m1fn).view(np.uint8) & 0xF
        words = c[..., 0::2] | (c[..., 1::2] << 4)
    return np.ascontiguousarray(words), np.ascontiguousarray(byte.astype(np.uint8).reshape(k // 512, 16, n))


def unpack_weight(words, scales, fmt):
    g, p, n, _ = words.shape
    if fmt == "e4m3":
        vals = np.ascontiguousarray(words).view(ml_dtypes.float8_e4m3fn).astype(np.float64)
    else:
        nib = np.empty((g, p, n, 4), np.uint8)
        nib[..., 0::2] = words & 0xF
        nib[..., 1::2] = words >> 4
        vals = E2M1[nib]
    vals = vals * np.repeat(np.exp2(scales.astype(np.float64) - 127.0), 8, axis=1)[..., None]
    return vals.transpose(0, 1, 3, 2).reshape(g * 512, n)
def pack4(w):
    words, scales = pack_weight(w, "e2m1")
    return words.reshape(words.shape[0], 128, -1), scales


def unpack4(words, scales):
    return unpack_weight(words.reshape(words.shape[0], 128, -1, 2), scales, "e2m1")


N, C, P, D = 512, 128, 7, 1024
SCALE = 1.0 / np.sqrt(D)


def draw0():
    s, t = mx_kscale(D), mx_kscale(D)
    h = bf(np.random.standard_normal((N, D)) * s)
    w_q_words, w_q_scales = pack4((np.random.standard_normal((D, D)) * 1.6 / np.sqrt(D) / s * t[:, None]).T)
    b_q = bf(np.random.standard_normal(D) * 0.2 * t)
    w_k_words, w_k_scales = pack4((np.random.standard_normal((D, D)) * 1.6 / np.sqrt(D) / s / t[:, None]).T)
    b_k = bf(np.random.standard_normal(D) * 0.2 / t)
    return {"h": h,
            "w_q_words": w_q_words, "w_q_scales": w_q_scales,
            "b_q": b_q,
            "w_k_words": w_k_words, "w_k_scales": w_k_scales,
            "b_k": b_k}


def core(h, w_q_words, w_q_scales, b_q, w_k_words, w_k_scales, b_k):
    hq = mxq(f64(h), 1, "e4m3")
    q = (hq @ unpack4(w_q_words, w_q_scales)) + f64(b_q)
    k = (hq @ unpack4(w_k_words, w_k_scales)) + f64(b_k)
    return (mxq(q, 1, "e4m3") @ mxq(k.T, 0, "e4m3")) * SCALE


def e4m3fn_bytes(y):
    return np.clip(np.asarray(y, np.float64), -448.0, 448.0).astype(np.float32).astype(ml_dtypes.float8_e4m3fn).view(np.uint8)


def e4m3fn_values(b):
    return np.asarray(b, np.uint8).view(ml_dtypes.float8_e4m3fn).astype(np.float64)


def setup_inputs():
    d = draw0()
    x0 = np.asarray(d['h']).astype(np.float64)
    s = (np.max(np.abs(x0), axis=(0,), keepdims=True) / 448.0).astype(np.float32)
    out = {}
    for k, v in d.items():
        if k == 'h':
            out['h_bytes'] = e4m3fn_bytes(x0 / s.astype(np.float64))
            out['h_scale'] = s
        else:
            out[k] = v
    return out


def reference(h_bytes, h_scale, w_q_words, w_q_scales, b_q, w_k_words, w_k_scales, b_k):
    return core(e4m3fn_values(h_bytes) * h_scale.astype(np.float64), w_q_words, w_q_scales, b_q, w_k_words, w_k_scales, b_k)

@@ -1,0 +1,304 @@
+from contextlib import ExitStack
+
+import concourse.mybir as mybir
+from concourse.masks import make_identity
+
+F32 = mybir.dt.float32
+BF16 = mybir.dt.bfloat16
+I32 = mybir.dt.int32
+U32 = mybir.dt.uint32
+U8 = mybir.dt.uint8
+FP8 = mybir.dt.float8_e4m3fn
+FP8X4 = mybir.dt.float8_e4m3fn_x4
+FP4X4 = mybir.dt.float4_e2m1fn_x4
+ACT = mybir.ActivationFunctionType
+ALU = mybir.AluOpType
+
+N, D, P = 512, 1024, 128
+FLOPS = 2 * (2 * N * D * D) + 2 * N * N * D
+RT = N // P
+SCALE = 0.03125
+
+
+def tile_selsahead_pb_w4_kernel(tc, h_bytes, h_scale, w_q_words, w_q_scales, b_q, w_k_words, w_k_scales, b_k, out):
+    nc = tc.nc
+    with ExitStack() as ctx:
+        keep = ctx.enter_context(tc.tile_pool(name="keep", bufs=1))
+        work = ctx.enter_context(tc.tile_pool(name="work", bufs=4))
+        psum = ctx.enter_context(tc.psum_pool(name="psum", bufs=1))
+        ctx.enter_context(nc.allow_non_contiguous_dma(reason="16-byte runs of small vectors"))
+
+        def bank(n):
+            return psum.tile([P, 512], F32, name="bank%d" % n)
+
+        ident = keep.tile([P, P], F32, name="ident")
+        hb = keep.tile([P, RT, D], U8, name="hb", align_bytes=64)
+        hx = [keep.tile([P, D], BF16, name="hx%d" % i, align_bytes=64) for i in range(RT)]
+        hs = keep.tile([P, 2, 4], F32, name="hs")
+        hq = keep.tile([P, 2, N], U32, name="hq", align_bytes=64)
+        hqs = keep.tile([P, 2, N], U8, name="hqs", align_bytes=64)
+        wst = [keep.tile([P, 4096], U8, name="wst%d" % m, align_bytes=64) for m in range(2)]
+        sst = [keep.tile([P, 2048], U8, name="sst%d" % m, align_bytes=64) for m in range(2)]
+        wp = [keep.tile([P, 4096], U8, name="wp%d" % m, align_bytes=64) for m in range(2)]
+        sp = [keep.tile([P, 2048], U8, name="sp%d" % m, align_bytes=64) for m in range(2)]
+        brow = keep.tile([P, 2 * P], BF16, name="brow")
+        brow32 = keep.tile([P, 2 * P], F32, name="brow32")
+        bias = keep.tile([P, 16], F32, name="bias")
+        zq = [keep.tile([P, 2, N], U32, name="zq%d" % m, align_bytes=64) for m in range(2)]
+        zqs = [keep.tile([P, 2, N], U8, name="zqs%d" % m, align_bytes=64) for m in range(2)]
+        ev = [[keep.tile([P, 4, N], BF16, name="ev%d%d" % (m, g), align_bytes=64) for g in range(2)] for m in range(2)]
+        osb = [keep.tile([P, N], F32, name="osb%d" % i) for i in range(RT)]
+        tiny = keep.tile([P, 1], F32, name="tiny")
+        tiny2 = keep.tile([P, 1], F32, name="tiny2")
+
+        words_in = [w_k_words, w_q_words]
+        scales_in = [w_k_scales, w_q_scales]
+        bias_in = [b_k, b_q]
+
+        def load_scales(m):
+            src = scales_in[m].bitcast(I32)
+            dst = sst[m][:].bitcast(I32).rearrange("p (a c) -> p a c", a=2)
+            for quad in range(4):
+                nc.sync.dma_start(out=dst[32 * quad : 32 * quad + 4], in_=src[:, 4 * quad : 4 * quad + 4, :].rearrange("a q c -> q a c"))
+
+        def load_words(m, g):
+            src = words_in[m].bitcast(I32)
+            dst = wst[m][:].bitcast(I32).rearrange("p (a c) -> p a c", a=2)
+            cols = slice(256 * g, 256 * g + 256)
+            nc.sync.dma_start(out=dst[:, :, cols], in_=src[:, :, cols].rearrange("a p c -> p a c"))
+
+        def permute_words(m, g):
+            src = wst[m][:].bitcast(I32).rearrange("p (a g q s w) -> p g a s q w", a=2, g=2, q=16, s=4)
+            dst = wp[m][:].bitcast(I32).rearrange("p (a g s q w) -> p g a s q w", a=2, g=2, q=16, s=4)
+            nc.vector.tensor_copy(out=dst[:, g], in_=src[:, g])
+
+        def permute_scales(m, g):
+            src = sst[m][:].bitcast(I32).rearrange("p (a g q s w) -> p g a s q w", a=2, g=2, q=16, s=4)
+            dst = sp[m][:].bitcast(I32).rearrange("p (a g s q w) -> p g a s q w", a=2, g=2, q=16, s=4)
+            nc.vector.tensor_copy(out=dst[:, g], in_=src[:, g])
+
+        def transpose_h(i, b):
+            words = hx[i][:].bitcast(F32)
+            for g in range(2):
+                for u in range(2):
+                    c = (2 * g + u) * P
+                    nc.tensor.transpose(b[:, c : c + P], words[:, 256 * g + u : 256 * (g + 1) : 2], ident[:])
+
+        def scale_h(i, g, b):
+            t = work.tile([P, 4 * P], BF16, name="hgrp", align_bytes=64)
+            src = b[:, 256 * g : 256 * g + 256].bitcast(BF16).rearrange("p (u n e) -> p n u e", u=2, e=2)
+            dst = t[:].rearrange("p (n u e) -> p n u e", u=2, e=2)
+            fac = hs[:, g, :].rearrange("p (u e) -> p u e", u=2).unsqueeze(1).to_broadcast([P, P, 2, 2])
+            nc.vector.tensor_tensor(out=dst, in0=src, in1=fac, op=ALU.mult)
+            return t
+
+        def quant_h(i, g, t):
+            cols = slice(P * i, P * i + P)
+            nc.vector.quantize_mx(out=hq[:, g, cols].bitcast(FP8X4), scales=hqs[:, g, cols], in_=t[:])
+
+        def project(m, g, s, cols, dst):
+            for a in range(2):
+                j = (a * 2 + g) * 4 + s
+                nc.tensor.matmul_mx(
+                    out=dst,
+                    lhsT=wp[m][:, 256 * j : 256 * j + 256].bitcast(FP4X4),
+                    lhsT_scale=sp[m][:, P * j : P * j + P],
+                    rhs=hq[:, a, cols].bitcast(FP8X4),
+                    rhs_scale=hqs[:, a, cols],
+                    start=(a == 0),
+                    stop=(a == 1),
+                )
+
+        def project_tile(m, g, i, b):
+            for s in range(4):
+                project(m, g, s, slice(P * i, P * i + P), b[:, P * s : P * s + P])
+
+        def bias_col(m, g, s):
+            j = g * 8 + m * 4 + s
+            return bias[:, j : j + 1]
+
+        def project_pair(m, g, h, s2, b):
+            for i in range(2):
+                for s in range(2):
+                    c = 256 * s + P * i
+                    project(m, g, 2 * s2 + s, slice(256 * h + P * i, 256 * h + P * i + P), b[:, c : c + P])
+
+        def evac_pair(m, g, h, s2, b):
+            for s in range(2):
+                nc.scalar.activation(out=ev[m][g][:, 2 * s2 + s, 256 * h : 256 * h + 256], in_=b[:, 256 * s : 256 * s + 256], func=ACT.Identity, bias=bias_col(m, g, 2 * s2 + s))
+
+        def fuse(m, g, i, b):
+            t = work.tile([P, 4 * P], BF16, name="zgrp128", align_bytes=64)
+            nc.vector.tensor_tensor(
+                out=t[:].rearrange("p (n s) -> p n s", s=4),
+                in0=b[:].rearrange("p (s n) -> p n s", s=4),
+                in1=bias[:, 8 * g + 4 * m : 8 * g + 4 * m + 4].unsqueeze(1).to_broadcast([P, P, 4]),
+                op=ALU.add,
+            )
+            return t
+
+        def evac_tile(m, g, i, b):
+            for s in range(4):
+                nc.scalar.activation(out=ev[m][g][:, s, P * i : P * i + P], in_=b[:, P * s : P * s + P], func=ACT.Identity, bias=bias_col(m, g, s))
+
+        def interleave(m, g, n0, n1):
+            t = work.tile([P, 4 * (n1 - n0)], BF16, name="zgrp%d" % (n1 - n0), align_bytes=64)
+            nc.vector.tensor_copy(out=t[:].rearrange("p (n s) -> p n s", s=4), in_=ev[m][g][:, :, n0:n1].rearrange("p s n -> p n s"))
+            return t
+
+        def quant_z(m, g, n0, n1, t):
+            nc.vector.quantize_mx(out=zq[m][:, g, n0:n1].bitcast(FP8X4), scales=zqs[m][:, g, n0:n1], in_=t[:])
+
+        def logits(i, b, g):
+            rows = slice(P * i, P * i + P)
+            nc.tensor.matmul_mx(
+                out=b[:],
+                lhsT=zq[1][:, g, rows].bitcast(FP8X4),
+                lhsT_scale=zqs[1][:, g, rows],
+                rhs=zq[0][:, g, :].bitcast(FP8X4),
+                rhs_scale=zqs[0][:, g, :],
+                start=(g == 0),
+                stop=(g == 1),
+            )
+
+        with tc.manual_schedule():
+            nc.scalar.dma_start(out=hs[:], in_=h_scale.rearrange("o (g p t) -> p (o g) t", g=2, t=4))
+            nc.vector.memset(tiny[:], 0.0)
+            nc.scalar.activation(out=tiny2[:], in_=tiny[:], func=ACT.Identity)
+            hsrc = h_bytes.rearrange("(i p) k -> p i k", p=P)
+            for i in range(2):
+                nc.sync.dma_start(out=hb[:, i, :], in_=hsrc[:, i, :])
+            nc.vector.memset(brow[:], 0.0)
+            for m in range(2):
+                nc.vector.memset(sst[m][:].bitcast(I32), 0)
+            load_scales(0)
+            load_words(0, 0)
+            nc.sync.dma_start(out=hb[:, 2:4, :], in_=hsrc[:, 2:4, :])
+            load_words(0, 1)
+            load_scales(1)
+            load_words(1, 0)
+            load_words(1, 1)
+            make_identity(nc, ident[:])
+            for m in range(2):
+                nc.gpsimd.dma_start(
+                    out=brow[4 * m : 4 * m + 4, :].rearrange("s (q r) -> s q r", r=8),
+                    in_=bias_in[m].rearrange("(q s r) -> s q r", q=32, s=4),
+                )
+
+            for half in range(2):
+                cols = slice(512 * half, 512 * half + 512)
+                nc.vector.tensor_copy(out=hx[0][:, cols], in_=hb[:, 0, cols].bitcast(FP8))
+            permute_words(0, 0)
+            permute_scales(0, 0)
+            for i in range(1, 3):
+                nc.scalar.copy(out=hx[i][:], in_=hb[:, i, :].bitcast(FP8))
+            nc.scalar.copy(out=hx[3][:], in_=hb[:, 3, :].bitcast(FP8))
+            nc.scalar.copy(out=brow32[:], in_=brow[:])
+            tb = [None] * 4
+            for i in range(3):
+                tb[i] = bank(i)
+                transpose_h(i, tb[i])
+
+            t00 = scale_h(0, 0, tb[0])
+            t01 = scale_h(0, 1, tb[0])
+            quant_h(0, 0, t00)
+            t10 = scale_h(1, 0, tb[1])
+            quant_h(0, 1, t01)
+            kb = {}
+            kb[0, 0] = bank(4)
+            project_tile(0, 0, 0, kb[0, 0])
+            tb[3] = bank(3)
+            transpose_h(3, tb[3])
+            bb = bank(6)
+            for g in range(2):
+                nc.tensor.transpose(bb[:, P * g : P * g + P], brow32[:, P * g : P * g + P], ident[:])
+            nc.scalar.copy(out=bias[:].rearrange("p (g c) -> p g c", g=2), in_=bb[:, 0:256].rearrange("p (g c) -> p g c", g=2)[:, :, 0:8])
+            permute_words(0, 1)
+            permute_scales(0, 1)
+            t11 = scale_h(1, 1, tb[1])
+            quant_h(1, 0, t10)
+            kb[0, 1] = bank(5)
+            project_tile(0, 1, 0, kb[0, 1])
+            t20 = scale_h(2, 0, tb[2])
+            quant_h(1, 1, t11)
+            evac_tile(0, 0, 0, kb[0, 0])
+            evac_tile(0, 1, 0, kb[0, 1])
+            for g in range(2):
+                kb[1, g] = bank(6 + g)
+                project_tile(0, g, 1, kb[1, g])
+                evac_tile(0, g, 1, kb[1, g])
+            t21 = scale_h(2, 1, tb[2])
+            quant_h(2, 0, t20)
+            t30 = scale_h(3, 0, tb[3])
+            quant_h(2, 1, t21)
+            t31 = scale_h(3, 1, tb[3])
+            quant_h(3, 0, t30)
+            permute_words(1, 0)
+            permute_scales(1, 0)
+            quant_h(3, 1, t31)
+            kbanks = [[0, 1], [4, 5]]
+            for i in range(2):
+                for g in range(2):
+                    kb[2 + i, g] = bank(kbanks[i][g])
+                    project_tile(0, g, 2 + i, kb[2 + i, g])
+                    if i == 0:
+                        evac_tile(0, g, 2, kb[2, g])
+            qbanks = [[2, 3, 6, 7], [0, 1, 4, 5]]
+            for g in range(2):
+                for s in range(4):
+                    b = bank(qbanks[g][s])
+                    if g == 0:
+                        project(1, g, s, slice(0, N), b[:])
+                        nc.scalar.activation(out=ev[1][g][:, s, :], in_=b[:], func=ACT.Identity, bias=bias_col(1, g, s))
+                    else:
+                        project_pair(1, g, s // 2, s % 2, b)
+                        evac_pair(1, g, s // 2, s % 2, b)
+                if g == 0:
+                    ka = interleave(0, 0, 0, 256)
+                    f30 = fuse(0, 0, 3, kb[3, 0])
+                    quant_z(0, 0, 0, 256, ka)
+                    f31 = fuse(0, 1, 3, kb[3, 1])
+                    quant_z(0, 0, 384, 512, f30)
+                    permute_words(1, 1)
+                    permute_scales(1, 1)
+                    quant_z(0, 1, 384, 512, f31)
+                    kb1 = interleave(0, 1, 0, 256)
+                    kc = interleave(0, 0, 256, 384)
+                    quant_z(0, 1, 0, 256, kb1)
+                    kd = interleave(0, 1, 256, 384)
+                    quant_z(0, 0, 256, 384, kc)
+            obanks = [2, 3, 6, 7]
+            ob = {}
+            q0a = interleave(1, 0, 0, 256)
+            quant_z(0, 1, 256, 384, kd)
+            q1a = interleave(1, 1, 0, 256)
+            quant_z(1, 0, 0, 256, q0a)
+            q0b = interleave(1, 0, 256, 512)
+            quant_z(1, 1, 0, 256, q1a)
+
+            def store(i, scalar_cols):
+                rows = slice(P * i, P * i + P)
+                if scalar_cols:
+                    nc.scalar.activation(out=osb[i][:, 0:scalar_cols], in_=ob[i][:, 0:scalar_cols], func=ACT.Copy, scale=SCALE)
+                    nc.sync.dma_start(out=out[rows, 0:scalar_cols], in_=osb[i][:, 0:scalar_cols])
+                if scalar_cols < N:
+                    nc.vector.tensor_scalar(out=osb[i][:, scalar_cols:N], in0=ob[i][:, scalar_cols:N], scalar1=SCALE, scalar2=None, op0=ALU.mult)
+                    nc.sync.dma_start(out=out[rows, scalar_cols:N], in_=osb[i][:, scalar_cols:N])
+
+            for i in range(2):
+                ob[i] = bank(obanks[i])
+                logits(i, ob[i], 0)
+                logits(i, ob[i], 1)
+                store(i, N)
+            q1b = interleave(1, 1, 256, 384)
+            quant_z(1, 0, 256, 512, q0b)
+            for i in range(2, RT):
+                ob[i] = bank(obanks[i])
+                logits(i, ob[i], 0)
+            q1c = interleave(1, 1, 384, 512)
+            quant_z(1, 1, 256, 384, q1b)
+            logits(2, ob[2], 1)
+            store(2, N)
+            quant_z(1, 1, 384, 512, q1c)
+            logits(3, ob[3], 1)
+            store(3, 256)

@@ -48,6 +48,7 @@ def tile_selsahead_pb_w4_kernel(tc, h_bytes, h_scale, w_q_words, w_q_scales, b_q
         zqs = [keep.tile([P, 2, N], U8, name="zqs%d" % m, align_bytes=64) for m in range(2)]
         ev = [[keep.tile([P, 4, N], BF16, name="ev%d%d" % (m, g), align_bytes=64) for g in range(2)] for m in range(2)]
         osb = [keep.tile([P, N], F32, name="osb%d" % i) for i in range(RT)]
+        warm = keep.tile([P, 512], BF16, name="warm")
         tiny = keep.tile([P, 1], F32, name="tiny")
         tiny2 = keep.tile([P, 1], F32, name="tiny2")
 
@@ -166,33 +167,34 @@ def tile_selsahead_pb_w4_kernel(tc, h_bytes, h_scale, w_q_words, w_q_scales, b_q
             nc.vector.memset(tiny[:], 0.0)
             nc.scalar.activation(out=tiny2[:], in_=tiny[:], func=ACT.Identity)
             hsrc = h_bytes.rearrange("(i p) k -> p i k", p=P)
-            for i in range(2):
-                nc.sync.dma_start(out=hb[:, i, :], in_=hsrc[:, i, :])
+            for c in [(0, 1), (1, 2), (2, 4)]:
+                nc.sync.dma_start(out=hb[:, c[0] : c[1], :], in_=hsrc[:, c[0] : c[1], :])
+            nc.vector.memset(sst[0][:].bitcast(I32), 0)
+            nc.vector.memset(warm[:], 0.0)
             nc.vector.memset(brow[:], 0.0)
-            for m in range(2):
-                nc.vector.memset(sst[m][:].bitcast(I32), 0)
+            nc.vector.memset(sst[1][:].bitcast(I32), 0)
             load_scales(0)
             load_words(0, 0)
-            nc.sync.dma_start(out=hb[:, 2:4, :], in_=hsrc[:, 2:4, :])
             load_words(0, 1)
+            for m in range(2):
+                nc.sync.dma_start(
+                    out=brow[4 * m : 4 * m + 4, :].rearrange("s (q r) -> s q r", r=8),
+                    in_=bias_in[m].rearrange("(q s r) -> s q r", q=32, s=4),
+                )
             load_scales(1)
             load_words(1, 0)
             load_words(1, 1)
             make_identity(nc, ident[:])
-            for m in range(2):
-                nc.gpsimd.dma_start(
-                    out=brow[4 * m : 4 * m + 4, :].rearrange("s (q r) -> s q r", r=8),
-                    in_=bias_in[m].rearrange("(q s r) -> s q r", q=32, s=4),
-                )
+
+            dummy = bank(7)
+            for i in range(4):
+                nc.tensor.matmul(dummy[:], warm[:, 0:P], warm[:], start=True, stop=True)
 
             for half in range(2):
                 cols = slice(512 * half, 512 * half + 512)
                 nc.vector.tensor_copy(out=hx[0][:, cols], in_=hb[:, 0, cols].bitcast(FP8))
-            permute_words(0, 0)
-            permute_scales(0, 0)
-            for i in range(1, 3):
+            for i in range(1, 4):
                 nc.scalar.copy(out=hx[i][:], in_=hb[:, i, :].bitcast(FP8))
-            nc.scalar.copy(out=hx[3][:], in_=hb[:, 3, :].bitcast(FP8))
             nc.scalar.copy(out=brow32[:], in_=brow[:])
             tb = [None] * 4
             for i in range(3):
@@ -204,6 +206,8 @@ def tile_selsahead_pb_w4_kernel(tc, h_bytes, h_scale, w_q_words, w_q_scales, b_q
             quant_h(0, 0, t00)
             t10 = scale_h(1, 0, tb[1])
             quant_h(0, 1, t01)
+            permute_words(0, 0)
+            permute_scales(0, 0)
             kb = {}
             kb[0, 0] = bank(4)
             project_tile(0, 0, 0, kb[0, 0])
@@ -213,10 +217,10 @@ def tile_selsahead_pb_w4_kernel(tc, h_bytes, h_scale, w_q_words, w_q_scales, b_q
             for g in range(2):
                 nc.tensor.transpose(bb[:, P * g : P * g + P], brow32[:, P * g : P * g + P], ident[:])
             nc.scalar.copy(out=bias[:].rearrange("p (g c) -> p g c", g=2), in_=bb[:, 0:256].rearrange("p (g c) -> p g c", g=2)[:, :, 0:8])
-            permute_words(0, 1)
-            permute_scales(0, 1)
             t11 = scale_h(1, 1, tb[1])
             quant_h(1, 0, t10)
+            permute_words(0, 1)
+            permute_scales(0, 1)
             kb[0, 1] = bank(5)
             project_tile(0, 1, 0, kb[0, 1])
             t20 = scale_h(2, 0, tb[2])

@@ -78,12 +78,15 @@ def tile_selsahead_pb_w4_kernel(tc, h_bytes, h_scale, w_q_words, w_q_scales, b_q
             dst = sp[m][:].bitcast(I32).rearrange("p (a g s q w) -> p g a s q w", a=2, g=2, q=16, s=4)
             nc.vector.tensor_copy(out=dst[:, g], in_=src[:, g])
 
-        def transpose_h(i, b):
+        def transpose_h(i, g, b):
             words = hx[i][:].bitcast(F32)
-            for g in range(2):
-                for u in range(2):
-                    c = (2 * g + u) * P
-                    nc.tensor.transpose(b[:, c : c + P], words[:, 256 * g + u : 256 * (g + 1) : 2], ident[:])
+            for u in range(2):
+                c = (2 * g + u) * P
+                nc.tensor.transpose(b[:, c : c + P], words[:, 256 * g + u : 256 * (g + 1) : 2], ident[:])
+
+        def warm_up(n):
+            for i in range(n):
+                nc.tensor.matmul(dummy[:], warm[:, 0:P], warm[:], start=True, stop=True)
 
         def scale_h(i, g, b):
             t = work.tile([P, 4 * P], BF16, name="hgrp", align_bytes=64)
@@ -144,7 +147,10 @@ def tile_selsahead_pb_w4_kernel(tc, h_bytes, h_scale, w_q_words, w_q_scales, b_q
 
         def interleave(m, g, n0, n1):
             t = work.tile([P, 4 * (n1 - n0)], BF16, name="zgrp%d" % (n1 - n0), align_bytes=64)
-            nc.vector.tensor_copy(out=t[:].rearrange("p (n s) -> p n s", s=4), in_=ev[m][g][:, :, n0:n1].rearrange("p s n -> p n s"))
+            nc.vector.tensor_copy(
+                out=t[:].rearrange("p (c i s) -> p c s i", i=4, s=4),
+                in_=ev[m][g][:, :, n0:n1].rearrange("p s (c i) -> p c s i", i=4),
+            )
             return t
 
         def quant_z(m, g, n0, n1, t):
@@ -162,6 +168,7 @@ def tile_selsahead_pb_w4_kernel(tc, h_bytes, h_scale, w_q_words, w_q_scales, b_q
                 stop=(g == 1),
             )
 
+        dummy = bank(6)
         with tc.manual_schedule():
             nc.scalar.dma_start(out=hs[:], in_=h_scale.rearrange("o (g p t) -> p (o g) t", g=2, t=4))
             nc.vector.memset(tiny[:], 0.0)
@@ -175,20 +182,18 @@ def tile_selsahead_pb_w4_kernel(tc, h_bytes, h_scale, w_q_words, w_q_scales, b_q
             nc.vector.memset(sst[1][:].bitcast(I32), 0)
             load_scales(0)
             load_words(0, 0)
-            load_words(0, 1)
             for m in range(2):
                 nc.sync.dma_start(
                     out=brow[4 * m : 4 * m + 4, :].rearrange("s (q r) -> s q r", r=8),
                     in_=bias_in[m].rearrange("(q s r) -> s q r", q=32, s=4),
                 )
+            load_words(0, 1)
             load_scales(1)
             load_words(1, 0)
             load_words(1, 1)
             make_identity(nc, ident[:])
 
-            dummy = bank(7)
-            for i in range(4):
-                nc.tensor.matmul(dummy[:], warm[:, 0:P], warm[:], start=True, stop=True)
+            warm_up(4)
 
             for half in range(2):
                 cols = slice(512 * half, 512 * half + 512)
@@ -196,34 +201,37 @@ def tile_selsahead_pb_w4_kernel(tc, h_bytes, h_scale, w_q_words, w_q_scales, b_q
             for i in range(1, 4):
                 nc.scalar.copy(out=hx[i][:], in_=hb[:, i, :].bitcast(FP8))
             nc.scalar.copy(out=brow32[:], in_=brow[:])
-            tb = [None] * 4
-            for i in range(3):
-                tb[i] = bank(i)
-                transpose_h(i, tb[i])
+            tb = {}
+            tb[0, 0] = bank(0)
+            tb[0, 1] = bank(7)
+            for i in range(1, 4):
+                tb[i, 0] = tb[i, 1] = bank(i)
+            for i in range(4):
+                for g in range(2):
+                    transpose_h(i, g, tb[i, g])
+                warm_up([1, 2, 1, 0][i])
+            bb = bank(5)
+            for g in range(2):
+                nc.tensor.transpose(bb[:, P * g : P * g + P], brow32[:, P * g : P * g + P], ident[:])
+            nc.scalar.copy(out=bias[:].rearrange("p (g c) -> p g c", g=2), in_=bb[:, 0:256].rearrange("p (g c) -> p g c", g=2)[:, :, 0:8])
 
-            t00 = scale_h(0, 0, tb[0])
-            t01 = scale_h(0, 1, tb[0])
+            t00 = scale_h(0, 0, tb[0, 0])
+            t01 = scale_h(0, 1, tb[0, 1])
             quant_h(0, 0, t00)
-            t10 = scale_h(1, 0, tb[1])
+            t10 = scale_h(1, 0, tb[1, 0])
             quant_h(0, 1, t01)
             permute_words(0, 0)
             permute_scales(0, 0)
             kb = {}
             kb[0, 0] = bank(4)
             project_tile(0, 0, 0, kb[0, 0])
-            tb[3] = bank(3)
-            transpose_h(3, tb[3])
-            bb = bank(6)
-            for g in range(2):
-                nc.tensor.transpose(bb[:, P * g : P * g + P], brow32[:, P * g : P * g + P], ident[:])
-            nc.scalar.copy(out=bias[:].rearrange("p (g c) -> p g c", g=2), in_=bb[:, 0:256].rearrange("p (g c) -> p g c", g=2)[:, :, 0:8])
-            t11 = scale_h(1, 1, tb[1])
+            t11 = scale_h(1, 1, tb[1, 1])
             quant_h(1, 0, t10)
             permute_words(0, 1)
             permute_scales(0, 1)
             kb[0, 1] = bank(5)
             project_tile(0, 1, 0, kb[0, 1])
-            t20 = scale_h(2, 0, tb[2])
+            t20 = scale_h(2, 0, tb[2, 0])
             quant_h(1, 1, t11)
             evac_tile(0, 0, 0, kb[0, 0])
             evac_tile(0, 1, 0, kb[0, 1])
@@ -231,11 +239,11 @@ def tile_selsahead_pb_w4_kernel(tc, h_bytes, h_scale, w_q_words, w_q_scales, b_q
                 kb[1, g] = bank(6 + g)
                 project_tile(0, g, 1, kb[1, g])
                 evac_tile(0, g, 1, kb[1, g])
-            t21 = scale_h(2, 1, tb[2])
+            t21 = scale_h(2, 1, tb[2, 1])
             quant_h(2, 0, t20)
-            t30 = scale_h(3, 0, tb[3])
+            t30 = scale_h(3, 0, tb[3, 0])
             quant_h(2, 1, t21)
-            t31 = scale_h(3, 1, tb[3])
+            t31 = scale_h(3, 1, tb[3, 1])
             quant_h(3, 0, t30)
             permute_words(1, 0)
             permute_scales(1, 0)
@@ -245,8 +253,8 @@ def tile_selsahead_pb_w4_kernel(tc, h_bytes, h_scale, w_q_words, w_q_scales, b_q
                 for g in range(2):
                     kb[2 + i, g] = bank(kbanks[i][g])
                     project_tile(0, g, 2 + i, kb[2 + i, g])
-                    if i == 0:
-                        evac_tile(0, g, 2, kb[2, g])
+                    if i == 0 or g == 0:
+                        evac_tile(0, g, 2 + i, kb[2 + i, g])
             qbanks = [[2, 3, 6, 7], [0, 1, 4, 5]]
             for g in range(2):
                 for s in range(4):
@@ -259,22 +267,20 @@ def tile_selsahead_pb_w4_kernel(tc, h_bytes, h_scale, w_q_words, w_q_scales, b_q
                         evac_pair(1, g, s // 2, s % 2, b)
                 if g == 0:
                     ka = interleave(0, 0, 0, 256)
-                    f30 = fuse(0, 0, 3, kb[3, 0])
+                    kb1 = interleave(0, 1, 0, 256)
                     quant_z(0, 0, 0, 256, ka)
-                    f31 = fuse(0, 1, 3, kb[3, 1])
-                    quant_z(0, 0, 384, 512, f30)
                     permute_words(1, 1)
                     permute_scales(1, 1)
-                    quant_z(0, 1, 384, 512, f31)
-                    kb1 = interleave(0, 1, 0, 256)
-                    kc = interleave(0, 0, 256, 384)
                     quant_z(0, 1, 0, 256, kb1)
                     kd = interleave(0, 1, 256, 384)
-                    quant_z(0, 0, 256, 384, kc)
+                    f31 = fuse(0, 1, 3, kb[3, 1])
+                    quant_z(0, 1, 256, 384, kd)
+                    kc = interleave(0, 0, 256, 512)
+                    quant_z(0, 1, 384, 512, f31)
             obanks = [2, 3, 6, 7]
             ob = {}
             q0a = interleave(1, 0, 0, 256)
-            quant_z(0, 1, 256, 384, kd)
+            quant_z(0, 0, 256, 512, kc)
             q1a = interleave(1, 1, 0, 256)
             quant_z(1, 0, 0, 256, q0a)
             q0b = interleave(1, 0, 256, 512)

@@ -42,7 +42,7 @@ def tile_selsahead_pb_w4_kernel(tc, h_bytes, h_scale, w_q_words, w_q_scales, b_q
         wp = [keep.tile([P, 4096], U8, name="wp%d" % m, align_bytes=64) for m in range(2)]
         sp = [keep.tile([P, 2048], U8, name="sp%d" % m, align_bytes=64) for m in range(2)]
         brow = keep.tile([P, 2 * P], BF16, name="brow")
-        brow32 = keep.tile([P, 2 * P], F32, name="brow32")
+        ident16 = keep.tile([P, P], BF16, name="ident16")
         bias = keep.tile([P, 16], F32, name="bias")
         zq = [keep.tile([P, 2, N], U32, name="zq%d" % m, align_bytes=64) for m in range(2)]
         zqs = [keep.tile([P, 2, N], U8, name="zqs%d" % m, align_bytes=64) for m in range(2)]
@@ -173,25 +173,27 @@ def tile_selsahead_pb_w4_kernel(tc, h_bytes, h_scale, w_q_words, w_q_scales, b_q
             nc.scalar.dma_start(out=hs[:], in_=h_scale.rearrange("o (g p t) -> p (o g) t", g=2, t=4))
             nc.vector.memset(tiny[:], 0.0)
             nc.scalar.activation(out=tiny2[:], in_=tiny[:], func=ACT.Identity)
-            hsrc = h_bytes.rearrange("(i p) k -> p i k", p=P)
-            for c in [(0, 1), (1, 2), (2, 4)]:
-                nc.sync.dma_start(out=hb[:, c[0] : c[1], :], in_=hsrc[:, c[0] : c[1], :])
             nc.vector.memset(sst[0][:].bitcast(I32), 0)
-            nc.vector.memset(warm[:], 0.0)
             nc.vector.memset(brow[:], 0.0)
+            nc.vector.memset(warm[:], 0.0)
             nc.vector.memset(sst[1][:].bitcast(I32), 0)
+            hsrc = h_bytes.rearrange("(i p) k -> p i k", p=P)
+            nc.sync.dma_start(out=hb[:, 0:1, :], in_=hsrc[:, 0:1, :])
+            nc.sync.dma_start(out=hb[:, 1:2, :], in_=hsrc[:, 1:2, :])
             load_scales(0)
-            load_words(0, 0)
+            nc.sync.dma_start(out=hb[:, 2:4, :], in_=hsrc[:, 2:4, :])
+            make_identity(nc, ident[:])
             for m in range(2):
-                nc.sync.dma_start(
+                nc.gpsimd.dma_start(
                     out=brow[4 * m : 4 * m + 4, :].rearrange("s (q r) -> s q r", r=8),
                     in_=bias_in[m].rearrange("(q s r) -> s q r", q=32, s=4),
                 )
+            load_words(0, 0)
             load_words(0, 1)
             load_scales(1)
             load_words(1, 0)
             load_words(1, 1)
-            make_identity(nc, ident[:])
+            nc.vector.tensor_copy(out=ident16[:], in_=ident[:])
 
             warm_up(4)
 
@@ -200,7 +202,6 @@ def tile_selsahead_pb_w4_kernel(tc, h_bytes, h_scale, w_q_words, w_q_scales, b_q
                 nc.vector.tensor_copy(out=hx[0][:, cols], in_=hb[:, 0, cols].bitcast(FP8))
             for i in range(1, 4):
                 nc.scalar.copy(out=hx[i][:], in_=hb[:, i, :].bitcast(FP8))
-            nc.scalar.copy(out=brow32[:], in_=brow[:])
             tb = {}
             tb[0, 0] = bank(0)
             tb[0, 1] = bank(7)
@@ -210,10 +211,10 @@ def tile_selsahead_pb_w4_kernel(tc, h_bytes, h_scale, w_q_words, w_q_scales, b_q
                 for g in range(2):
                     transpose_h(i, g, tb[i, g])
                 warm_up([1, 2, 1, 0][i])
-            bb = bank(5)
+            bb16 = bank(5)[:].bitcast(BF16)
             for g in range(2):
-                nc.tensor.transpose(bb[:, P * g : P * g + P], brow32[:, P * g : P * g + P], ident[:])
-            nc.scalar.copy(out=bias[:].rearrange("p (g c) -> p g c", g=2), in_=bb[:, 0:256].rearrange("p (g c) -> p g c", g=2)[:, :, 0:8])
+                nc.tensor.transpose(bb16[:, P * g : P * g + P], brow[:, P * g : P * g + P], ident16[:])
+            nc.scalar.copy(out=bias[:].rearrange("p (g c) -> p g c", g=2), in_=bb16[:, 0:256].rearrange("p (g c) -> p g c", g=2)[:, :, 0:8])
 
             t00 = scale_h(0, 0, tb[0, 0])
             t01 = scale_h(0, 1, tb[0, 1])
@@ -246,15 +247,13 @@ def tile_selsahead_pb_w4_kernel(tc, h_bytes, h_scale, w_q_words, w_q_scales, b_q
             t31 = scale_h(3, 1, tb[3, 1])
             quant_h(3, 0, t30)
             permute_words(1, 0)
-            permute_scales(1, 0)
             quant_h(3, 1, t31)
+            permute_scales(1, 0)
             kbanks = [[0, 1], [4, 5]]
-            for i in range(2):
-                for g in range(2):
-                    kb[2 + i, g] = bank(kbanks[i][g])
-                    project_tile(0, g, 2 + i, kb[2 + i, g])
-                    if i == 0 or g == 0:
-                        evac_tile(0, g, 2 + i, kb[2 + i, g])
+            for i, g in [(2, 0), (2, 1), (3, 0)]:
+                kb[i, g] = bank(kbanks[i - 2][g])
+                project_tile(0, g, i, kb[i, g])
+                evac_tile(0, g, i, kb[i, g])
             qbanks = [[2, 3, 6, 7], [0, 1, 4, 5]]
             for g in range(2):
                 for s in range(4):
@@ -266,6 +265,8 @@ def tile_selsahead_pb_w4_kernel(tc, h_bytes, h_scale, w_q_words, w_q_scales, b_q
                         project_pair(1, g, s // 2, s % 2, b)
                         evac_pair(1, g, s // 2, s % 2, b)
                 if g == 0:
+                    kb[3, 1] = bank(kbanks[1][1])
+                    project_tile(0, 1, 3, kb[3, 1])
                     ka = interleave(0, 0, 0, 256)
                     kb1 = interleave(0, 1, 0, 256)
                     quant_z(0, 0, 0, 256, ka)
@@ -273,33 +274,32 @@ def tile_selsahead_pb_w4_kernel(tc, h_bytes, h_scale, w_q_words, w_q_scales, b_q
                     permute_scales(1, 1)
                     quant_z(0, 1, 0, 256, kb1)
                     kd = interleave(0, 1, 256, 384)
-                    f31 = fuse(0, 1, 3, kb[3, 1])
-                    quant_z(0, 1, 256, 384, kd)
                     kc = interleave(0, 0, 256, 512)
-                    quant_z(0, 1, 384, 512, f31)
+                    quant_z(0, 1, 256, 384, kd)
+                    f31 = fuse(0, 1, 3, kb[3, 1])
+                    quant_z(0, 0, 256, 512, kc)
             obanks = [2, 3, 6, 7]
             ob = {}
             q0a = interleave(1, 0, 0, 256)
-            quant_z(0, 0, 256, 512, kc)
+            quant_z(0, 1, 384, 512, f31)
             q1a = interleave(1, 1, 0, 256)
             quant_z(1, 0, 0, 256, q0a)
-            q0b = interleave(1, 0, 256, 512)
             quant_z(1, 1, 0, 256, q1a)
+            q0b = interleave(1, 0, 256, 512)
 
-            def store(i, scalar_cols):
+            def store(i, split):
                 rows = slice(P * i, P * i + P)
-                if scalar_cols:
-                    nc.scalar.activation(out=osb[i][:, 0:scalar_cols], in_=ob[i][:, 0:scalar_cols], func=ACT.Copy, scale=SCALE)
-                    nc.sync.dma_start(out=out[rows, 0:scalar_cols], in_=osb[i][:, 0:scalar_cols])
-                if scalar_cols < N:
-                    nc.vector.tensor_scalar(out=osb[i][:, scalar_cols:N], in0=ob[i][:, scalar_cols:N], scalar1=SCALE, scalar2=None, op0=ALU.mult)
-                    nc.sync.dma_start(out=out[rows, scalar_cols:N], in_=osb[i][:, scalar_cols:N])
+                cut = N // 2 if split else N
+                nc.scalar.activation(out=osb[i][:, 0:cut], in_=ob[i][:, 0:cut], func=ACT.Copy, scale=SCALE)
+                if split:
+                    nc.vector.tensor_scalar(out=osb[i][:, cut:N], in0=ob[i][:, cut:N], scalar1=SCALE, scalar2=None, op0=ALU.mult)
+                nc.sync.dma_start(out=out[rows, :], in_=osb[i][:])
 
             for i in range(2):
                 ob[i] = bank(obanks[i])
                 logits(i, ob[i], 0)
                 logits(i, ob[i], 1)
-                store(i, N)
+                store(i, False)
             q1b = interleave(1, 1, 256, 384)
             quant_z(1, 0, 256, 512, q0b)
             for i in range(2, RT):
@@ -307,8 +307,8 @@ def tile_selsahead_pb_w4_kernel(tc, h_bytes, h_scale, w_q_words, w_q_scales, b_q
                 logits(i, ob[i], 0)
             q1c = interleave(1, 1, 384, 512)
             quant_z(1, 1, 256, 384, q1b)
-            logits(2, ob[2], 1)
-            store(2, N)
             quant_z(1, 1, 384, 512, q1c)
+            logits(2, ob[2], 1)
+            store(2, True)
             logits(3, ob[3], 1)
-            store(3, 256)
+            store(3, True)

@@ -37,16 +37,18 @@ def tile_selsahead_pb_w4_kernel(tc, h_bytes, h_scale, w_q_words, w_q_scales, b_q
         hs = keep.tile([P, 2, 4], F32, name="hs")
         hq = keep.tile([P, 2, N], U32, name="hq", align_bytes=64)
         hqs = keep.tile([P, 2, N], U8, name="hqs", align_bytes=64)
-        wst = [keep.tile([P, 4096], U8, name="wst%d" % m, align_bytes=64) for m in range(2)]
+        wst = [[keep.tile([P, 2048], U8, name="wst%d%d" % (m, g), align_bytes=64) for g in range(2)] for m in range(2)]
         sst = [keep.tile([P, 2048], U8, name="sst%d" % m, align_bytes=64) for m in range(2)]
-        wp = [keep.tile([P, 4096], U8, name="wp%d" % m, align_bytes=64) for m in range(2)]
-        sp = [keep.tile([P, 2048], U8, name="sp%d" % m, align_bytes=64) for m in range(2)]
+        wp = [[keep.tile([P, 2048], U8, name="wp%d%d" % (m, g), align_bytes=64) for g in range(2)] for m in range(2)]
+        sp = [[keep.tile([P, 1024], U8, name="sp%d%d" % (m, g), align_bytes=64) for g in range(2)] for m in range(2)]
         brow = keep.tile([P, 2 * P], BF16, name="brow")
         ident16 = keep.tile([P, P], BF16, name="ident16")
         bias = keep.tile([P, 16], F32, name="bias")
         zq = [keep.tile([P, 2, N], U32, name="zq%d" % m, align_bytes=64) for m in range(2)]
         zqs = [keep.tile([P, 2, N], U8, name="zqs%d" % m, align_bytes=64) for m in range(2)]
-        ev = [[keep.tile([P, 4, N], BF16, name="ev%d%d" % (m, g), align_bytes=64) for g in range(2)] for m in range(2)]
+        evk = [keep.tile([P, RT, 4, P], BF16, name="evk%d" % g, align_bytes=64) for g in range(2)]
+        evq0 = keep.tile([P, 4, N], BF16, name="evq0", align_bytes=64)
+        evq1 = keep.tile([P, 2, 4, 256], BF16, name="evq1", align_bytes=64)
         osb = [keep.tile([P, N], F32, name="osb%d" % i) for i in range(RT)]
         warm = keep.tile([P, 512], BF16, name="warm")
         tiny = keep.tile([P, 1], F32, name="tiny")
@@ -64,19 +66,24 @@ def tile_selsahead_pb_w4_kernel(tc, h_bytes, h_scale, w_q_words, w_q_scales, b_q
 
         def load_words(m, g):
             src = words_in[m].bitcast(I32)
-            dst = wst[m][:].bitcast(I32).rearrange("p (a c) -> p a c", a=2)
-            cols = slice(256 * g, 256 * g + 256)
-            nc.sync.dma_start(out=dst[:, :, cols], in_=src[:, :, cols].rearrange("a p c -> p a c"))
+            dst = wst[m][g][:].bitcast(I32).rearrange("p (a c) -> p a c", a=2)
+            nc.sync.dma_start(out=dst, in_=src[:, :, 256 * g : 256 * g + 256].rearrange("a p c -> p a c"))
+
+        def load_bias(m):
+            nc.sync.dma_start(
+                out=brow[4 * m : 4 * m + 4, :].rearrange("s (q r) -> s q r", r=8),
+                in_=bias_in[m].rearrange("(q s r) -> s q r", q=32, s=4),
+            )
 
         def permute_words(m, g):
-            src = wst[m][:].bitcast(I32).rearrange("p (a g q s w) -> p g a s q w", a=2, g=2, q=16, s=4)
-            dst = wp[m][:].bitcast(I32).rearrange("p (a g s q w) -> p g a s q w", a=2, g=2, q=16, s=4)
-            nc.vector.tensor_copy(out=dst[:, g], in_=src[:, g])
+            src = wst[m][g][:].bitcast(I32).rearrange("p (a q s w) -> p a s q w", a=2, q=16, s=4)
+            dst = wp[m][g][:].bitcast(I32).rearrange("p (a s q w) -> p a s q w", a=2, q=16, s=4)
+            nc.vector.tensor_copy(out=dst, in_=src)
 
         def permute_scales(m, g):
             src = sst[m][:].bitcast(I32).rearrange("p (a g q s w) -> p g a s q w", a=2, g=2, q=16, s=4)
-            dst = sp[m][:].bitcast(I32).rearrange("p (a g s q w) -> p g a s q w", a=2, g=2, q=16, s=4)
-            nc.vector.tensor_copy(out=dst[:, g], in_=src[:, g])
+            dst = sp[m][g][:].bitcast(I32).rearrange("p (a s q w) -> p a s q w", a=2, q=16, s=4)
+            nc.vector.tensor_copy(out=dst, in_=src[:, g])
 
         def transpose_h(i, g, b):
             words = hx[i][:].bitcast(F32)
@@ -96,17 +103,32 @@ def tile_selsahead_pb_w4_kernel(tc, h_bytes, h_scale, w_q_words, w_q_scales, b_q
             nc.vector.tensor_tensor(out=dst, in0=src, in1=fac, op=ALU.mult)
             return t
 
+        def scale_h_planes(i, g, b):
+            ph = work.tile([P, 4, P], BF16, name="hplane", align_bytes=64)
+            src = b[:, 256 * g : 256 * g + 256].bitcast(BF16).rearrange("p (u n e) -> p u e n", u=2, e=2)
+            for t in range(4):
+                nc.scalar.activation(out=ph[:, t, :], in_=src[:, t // 2, t % 2], func=ACT.Copy, scale=hs[:, g, t : t + 1])
+            return ph
+
+        def weave_h(ph):
+            t = work.tile([P, 4 * P], BF16, name="hgrp", align_bytes=64)
+            nc.vector.tensor_copy(
+                out=t[:].rearrange("p (c i s) -> p c s i", i=4, s=4),
+                in_=ph[:].rearrange("p s (c i) -> p c s i", i=4),
+            )
+            return t
+
         def quant_h(i, g, t):
             cols = slice(P * i, P * i + P)
             nc.vector.quantize_mx(out=hq[:, g, cols].bitcast(FP8X4), scales=hqs[:, g, cols], in_=t[:])
 
         def project(m, g, s, cols, dst):
             for a in range(2):
-                j = (a * 2 + g) * 4 + s
+                j = a * 4 + s
                 nc.tensor.matmul_mx(
                     out=dst,
-                    lhsT=wp[m][:, 256 * j : 256 * j + 256].bitcast(FP4X4),
-                    lhsT_scale=sp[m][:, P * j : P * j + P],
+                    lhsT=wp[m][g][:, 256 * j : 256 * j + 256].bitcast(FP4X4),
+                    lhsT_scale=sp[m][g][:, P * j : P * j + P],
                     rhs=hq[:, a, cols].bitcast(FP8X4),
                     rhs_scale=hqs[:, a, cols],
                     start=(a == 0),
@@ -129,7 +151,7 @@ def tile_selsahead_pb_w4_kernel(tc, h_bytes, h_scale, w_q_words, w_q_scales, b_q
 
         def evac_pair(m, g, h, s2, b):
             for s in range(2):
-                nc.scalar.activation(out=ev[m][g][:, 2 * s2 + s, 256 * h : 256 * h + 256], in_=b[:, 256 * s : 256 * s + 256], func=ACT.Identity, bias=bias_col(m, g, 2 * s2 + s))
+                nc.scalar.activation(out=evq1[:, h, 2 * s2 + s, :], in_=b[:, 256 * s : 256 * s + 256], func=ACT.Identity, bias=bias_col(m, g, 2 * s2 + s))
 
         def fuse(m, g, i, b):
             t = work.tile([P, 4 * P], BF16, name="zgrp128", align_bytes=64)
@@ -141,16 +163,27 @@ def tile_selsahead_pb_w4_kernel(tc, h_bytes, h_scale, w_q_words, w_q_scales, b_q
             )
             return t
 
+        def evac_s(m, g, s, b):
+            nc.scalar.activation(out=evq0[:, s, :], in_=b[:], func=ACT.Identity, bias=bias_col(m, g, s))
+
+        def evac_v(m, g, s, b):
+            nc.vector.tensor_scalar(out=evq0[:, s, :], in0=b[:], scalar1=bias_col(m, g, s), scalar2=None, op0=ALU.add)
+
         def evac_tile(m, g, i, b):
             for s in range(4):
-                nc.scalar.activation(out=ev[m][g][:, s, P * i : P * i + P], in_=b[:, P * s : P * s + P], func=ACT.Identity, bias=bias_col(m, g, s))
+                nc.scalar.activation(out=evk[g][:, i, s, :], in_=b[:, P * s : P * s + P], func=ACT.Identity, bias=bias_col(m, g, s))
 
         def interleave(m, g, n0, n1):
             t = work.tile([P, 4 * (n1 - n0)], BF16, name="zgrp%d" % (n1 - n0), align_bytes=64)
-            nc.vector.tensor_copy(
-                out=t[:].rearrange("p (c i s) -> p c s i", i=4, s=4),
-                in_=ev[m][g][:, :, n0:n1].rearrange("p s (c i) -> p c s i", i=4),
-            )
+            if m == 0:
+                src = evk[g][:, n0 // P : n1 // P].rearrange("p b s (c i) -> p b c s i", i=4)
+                dst = t[:].rearrange("p (b c i s) -> p b c s i", b=(n1 - n0) // P, i=4, s=4)
+            else:
+                h = n0 // 256
+                rows = evq0[:, :, n0:n1] if g == 0 else evq1[:, h, :, n0 - 256 * h : n1 - 256 * h]
+                src = rows.rearrange("p s (c i) -> p c s i", i=4)
+                dst = t[:].rearrange("p (c i s) -> p c s i", i=4, s=4)
+            nc.vector.tensor_copy(out=dst, in_=src)
             return t
 
         def quant_z(m, g, n0, n1, t):
@@ -175,32 +208,30 @@ def tile_selsahead_pb_w4_kernel(tc, h_bytes, h_scale, w_q_words, w_q_scales, b_q
             nc.scalar.activation(out=tiny2[:], in_=tiny[:], func=ACT.Identity)
             nc.vector.memset(sst[0][:].bitcast(I32), 0)
             nc.vector.memset(brow[:], 0.0)
-            nc.vector.memset(warm[:], 0.0)
-            nc.vector.memset(sst[1][:].bitcast(I32), 0)
+            nc.gpsimd.memset(warm[:], 0.0)
+            make_identity(nc, ident[:])
+            nc.gpsimd.memset(sst[1][:].bitcast(I32), 0)
             hsrc = h_bytes.rearrange("(i p) k -> p i k", p=P)
             nc.sync.dma_start(out=hb[:, 0:1, :], in_=hsrc[:, 0:1, :])
             nc.sync.dma_start(out=hb[:, 1:2, :], in_=hsrc[:, 1:2, :])
-            load_scales(0)
             nc.sync.dma_start(out=hb[:, 2:4, :], in_=hsrc[:, 2:4, :])
-            make_identity(nc, ident[:])
-            for m in range(2):
-                nc.gpsimd.dma_start(
-                    out=brow[4 * m : 4 * m + 4, :].rearrange("s (q r) -> s q r", r=8),
-                    in_=bias_in[m].rearrange("(q s r) -> s q r", q=32, s=4),
-                )
+            load_scales(0)
             load_words(0, 0)
+            load_bias(0)
+            load_bias(1)
             load_words(0, 1)
             load_scales(1)
             load_words(1, 0)
             load_words(1, 1)
             nc.vector.tensor_copy(out=ident16[:], in_=ident[:])
 
-            warm_up(4)
+            warm_up(5)
 
             for half in range(2):
                 cols = slice(512 * half, 512 * half + 512)
                 nc.vector.tensor_copy(out=hx[0][:, cols], in_=hb[:, 0, cols].bitcast(FP8))
-            for i in range(1, 4):
+            nc.vector.tensor_copy(out=hx[1][:], in_=hb[:, 1, :].bitcast(FP8))
+            for i in range(2, 4):
                 nc.scalar.copy(out=hx[i][:], in_=hb[:, i, :].bitcast(FP8))
             tb = {}
             tb[0, 0] = bank(0)
@@ -211,104 +242,107 @@ def tile_selsahead_pb_w4_kernel(tc, h_bytes, h_scale, w_q_words, w_q_scales, b_q
                 for g in range(2):
                     transpose_h(i, g, tb[i, g])
                 warm_up([1, 2, 1, 0][i])
-            bb16 = bank(5)[:].bitcast(BF16)
+            ph20 = scale_h_planes(2, 0, tb[2, 0])
+            ph21 = scale_h_planes(2, 1, tb[2, 1])
+
+
+            t00 = scale_h(0, 0, tb[0, 0])
+            kb = {}
+            t01 = scale_h(0, 1, tb[0, 1])
+            quant_h(0, 0, t00)
+            permute_words(0, 0)
+            permute_scales(0, 0)
+            quant_h(0, 1, t01)
+            kb[0, 0] = bank(4)
+            project_tile(0, 0, 0, kb[0, 0])
+            bb16 = bank(6)[:].bitcast(BF16)
             for g in range(2):
                 nc.tensor.transpose(bb16[:, P * g : P * g + P], brow[:, P * g : P * g + P], ident16[:])
             nc.scalar.copy(out=bias[:].rearrange("p (g c) -> p g c", g=2), in_=bb16[:, 0:256].rearrange("p (g c) -> p g c", g=2)[:, :, 0:8])
-
-            t00 = scale_h(0, 0, tb[0, 0])
-            t01 = scale_h(0, 1, tb[0, 1])
-            quant_h(0, 0, t00)
+            evac_tile(0, 0, 0, kb[0, 0])
             t10 = scale_h(1, 0, tb[1, 0])
-            quant_h(0, 1, t01)
-            permute_words(0, 0)
-            permute_scales(0, 0)
-            kb = {}
-            kb[0, 0] = bank(4)
-            project_tile(0, 0, 0, kb[0, 0])
-            t11 = scale_h(1, 1, tb[1, 1])
-            quant_h(1, 0, t10)
             permute_words(0, 1)
             permute_scales(0, 1)
             kb[0, 1] = bank(5)
             project_tile(0, 1, 0, kb[0, 1])
-            t20 = scale_h(2, 0, tb[2, 0])
-            quant_h(1, 1, t11)
-            evac_tile(0, 0, 0, kb[0, 0])
             evac_tile(0, 1, 0, kb[0, 1])
-            for g in range(2):
-                kb[1, g] = bank(6 + g)
-                project_tile(0, g, 1, kb[1, g])
-                evac_tile(0, g, 1, kb[1, g])
-            t21 = scale_h(2, 1, tb[2, 1])
+            t11 = scale_h(1, 1, tb[1, 1])
+            quant_h(1, 0, t10)
+            t20 = weave_h(ph20)
+            quant_h(1, 1, t11)
+            kb[1, 0] = bank(6)
+            project_tile(0, 0, 1, kb[1, 0])
+            evac_tile(0, 0, 1, kb[1, 0])
+            kb[1, 1] = bank(7)
+            project_tile(0, 1, 1, kb[1, 1])
+            evac_tile(0, 1, 1, kb[1, 1])
+            t21 = weave_h(ph21)
             quant_h(2, 0, t20)
             t30 = scale_h(3, 0, tb[3, 0])
             quant_h(2, 1, t21)
+            kb[2, 0] = bank(0)
+            project_tile(0, 0, 2, kb[2, 0])
+            evac_tile(0, 0, 2, kb[2, 0])
+            kb[2, 1] = bank(1)
+            project_tile(0, 1, 2, kb[2, 1])
+            evac_tile(0, 1, 2, kb[2, 1])
             t31 = scale_h(3, 1, tb[3, 1])
             quant_h(3, 0, t30)
             permute_words(1, 0)
             quant_h(3, 1, t31)
+            kb[3, 0] = bank(4)
+            project_tile(0, 0, 3, kb[3, 0])
+            evac_tile(0, 0, 3, kb[3, 0])
             permute_scales(1, 0)
-            kbanks = [[0, 1], [4, 5]]
-            for i, g in [(2, 0), (2, 1), (3, 0)]:
-                kb[i, g] = bank(kbanks[i - 2][g])
-                project_tile(0, g, i, kb[i, g])
-                evac_tile(0, g, i, kb[i, g])
-            qbanks = [[2, 3, 6, 7], [0, 1, 4, 5]]
-            for g in range(2):
-                for s in range(4):
-                    b = bank(qbanks[g][s])
-                    if g == 0:
-                        project(1, g, s, slice(0, N), b[:])
-                        nc.scalar.activation(out=ev[1][g][:, s, :], in_=b[:], func=ACT.Identity, bias=bias_col(1, g, s))
-                    else:
-                        project_pair(1, g, s // 2, s % 2, b)
-                        evac_pair(1, g, s // 2, s % 2, b)
-                if g == 0:
-                    kb[3, 1] = bank(kbanks[1][1])
-                    project_tile(0, 1, 3, kb[3, 1])
-                    ka = interleave(0, 0, 0, 256)
-                    kb1 = interleave(0, 1, 0, 256)
-                    quant_z(0, 0, 0, 256, ka)
-                    permute_words(1, 1)
-                    permute_scales(1, 1)
-                    quant_z(0, 1, 0, 256, kb1)
-                    kd = interleave(0, 1, 256, 384)
-                    kc = interleave(0, 0, 256, 512)
-                    quant_z(0, 1, 256, 384, kd)
-                    f31 = fuse(0, 1, 3, kb[3, 1])
-                    quant_z(0, 0, 256, 512, kc)
-            obanks = [2, 3, 6, 7]
+            q0bank = [bank(2), bank(3), bank(6), bank(7)]
+            for s in range(4):
+                project(1, 0, s, slice(0, N), q0bank[s][:])
+            evac_s(1, 0, 0, q0bank[0])
+            evac_s(1, 0, 1, q0bank[1])
+            evac_s(1, 0, 3, q0bank[3])
+            ka = interleave(0, 0, 0, 256)
+            kb1 = interleave(0, 1, 0, 256)
+            quant_z(0, 0, 0, 256, ka)
+            permute_words(1, 1)
+            permute_scales(1, 1)
+            kb[3, 1] = bank(5)
+            project_tile(0, 1, 3, kb[3, 1])
+            for h in range(2):
+                for s2 in range(2):
+                    b = bank([[0, 1], [4, 2]][h][s2])
+                    project_pair(1, 1, h, s2, b)
+                    evac_pair(1, 1, h, s2, b)
             ob = {}
+            quant_z(0, 1, 0, 256, kb1)
+            kd = interleave(0, 1, 256, 384)
+            kc = interleave(0, 0, 256, 512)
+            quant_z(0, 1, 256, 384, kd)
+            evac_v(1, 0, 2, q0bank[2])
+            quant_z(0, 0, 256, 512, kc)
+            f31 = fuse(0, 1, 3, kb[3, 1])
             q0a = interleave(1, 0, 0, 256)
             quant_z(0, 1, 384, 512, f31)
-            q1a = interleave(1, 1, 0, 256)
-            quant_z(1, 0, 0, 256, q0a)
-            quant_z(1, 1, 0, 256, q1a)
             q0b = interleave(1, 0, 256, 512)
-
-            def store(i, split):
-                rows = slice(P * i, P * i + P)
-                cut = N // 2 if split else N
-                nc.scalar.activation(out=osb[i][:, 0:cut], in_=ob[i][:, 0:cut], func=ACT.Copy, scale=SCALE)
-                if split:
-                    nc.vector.tensor_scalar(out=osb[i][:, cut:N], in0=ob[i][:, cut:N], scalar1=SCALE, scalar2=None, op0=ALU.mult)
-                nc.sync.dma_start(out=out[rows, :], in_=osb[i][:])
-
+            quant_z(1, 0, 0, 256, q0a)
             for i in range(2):
-                ob[i] = bank(obanks[i])
+                ob[i] = bank([3, 6, 7, 0][i])
                 logits(i, ob[i], 0)
-                logits(i, ob[i], 1)
-                store(i, False)
-            q1b = interleave(1, 1, 256, 384)
+            q1a = interleave(1, 1, 0, 256)
             quant_z(1, 0, 256, 512, q0b)
             for i in range(2, RT):
-                ob[i] = bank(obanks[i])
+                ob[i] = bank([3, 6, 7, 0][i])
                 logits(i, ob[i], 0)
+            quant_z(1, 1, 0, 256, q1a)
+            q1b = interleave(1, 1, 256, 384)
             q1c = interleave(1, 1, 384, 512)
             quant_z(1, 1, 256, 384, q1b)
             quant_z(1, 1, 384, 512, q1c)
-            logits(2, ob[2], 1)
-            store(2, True)
-            logits(3, ob[3], 1)
-            store(3, True)
+            for i in range(RT):
+                logits(i, ob[i], 1)
+                rows = slice(P * i, P * i + P)
+                cut = [N // 2, N // 2, N // 2, N // 2][i]
+                if cut:
+                    nc.scalar.activation(out=osb[i][:, 0:cut], in_=ob[i][:, 0:cut], func=ACT.Copy, scale=SCALE)
+                if cut < N:
+                    nc.vector.tensor_scalar(out=osb[i][:, cut:N], in0=ob[i][:, cut:N], scalar1=SCALE, scalar2=None, op0=ALU.mult)
+                nc.sync.dma_start(out=out[rows, :], in_=osb[i][:])

from contextlib import ExitStack

import concourse.mybir as mybir
from concourse.masks import make_identity

F32 = mybir.dt.float32
BF16 = mybir.dt.bfloat16
I32 = mybir.dt.int32
U32 = mybir.dt.uint32
U8 = mybir.dt.uint8
FP8 = mybir.dt.float8_e4m3fn
FP8X4 = mybir.dt.float8_e4m3fn_x4
FP4X4 = mybir.dt.float4_e2m1fn_x4
ACT = mybir.ActivationFunctionType
ALU = mybir.AluOpType

N, D, P = 512, 1024, 128
FLOPS = 2 * (2 * N * D * D) + 2 * N * N * D
RT = N // P
SCALE = 0.03125


def tile_selsahead_pb_w4_kernel(tc, h_bytes, h_scale, w_q_words, w_q_scales, b_q, w_k_words, w_k_scales, b_k, out):
    nc = tc.nc
    with ExitStack() as ctx:
        keep = ctx.enter_context(tc.tile_pool(name="keep", bufs=1))
        work = ctx.enter_context(tc.tile_pool(name="work", bufs=4))
        psum = ctx.enter_context(tc.psum_pool(name="psum", bufs=1))
        ctx.enter_context(nc.allow_non_contiguous_dma(reason="16-byte runs of small vectors"))

        def bank(n):
            return psum.tile([P, 512], F32, name="bank%d" % n)

        ident = keep.tile([P, P], F32, name="ident")
        hb = keep.tile([P, RT, D], U8, name="hb", align_bytes=64)
        hx = [keep.tile([P, D], BF16, name="hx%d" % i, align_bytes=64) for i in range(RT)]
        hs = keep.tile([P, 2, 4], F32, name="hs")
        hq = keep.tile([P, 2, N], U32, name="hq", align_bytes=64)
        hqs = keep.tile([P, 2, N], U8, name="hqs", align_bytes=64)
        wst = [[keep.tile([P, 2048], U8, name="wst%d%d" % (m, g), align_bytes=64) for g in range(2)] for m in range(2)]
        sst = [keep.tile([P, 2048], U8, name="sst%d" % m, align_bytes=64) for m in range(2)]
        wp = [[keep.tile([P, 2048], U8, name="wp%d%d" % (m, g), align_bytes=64) for g in range(2)] for m in range(2)]
        sp = [[keep.tile([P, 1024], U8, name="sp%d%d" % (m, g), align_bytes=64) for g in range(2)] for m in range(2)]
        brow = keep.tile([P, 2 * P], BF16, name="brow")
        ident16 = keep.tile([P, P], BF16, name="ident16")
        bias = keep.tile([P, 16], F32, name="bias")
        zq = [keep.tile([P, 2, N], U32, name="zq%d" % m, align_bytes=64) for m in range(2)]
        zqs = [keep.tile([P, 2, N], U8, name="zqs%d" % m, align_bytes=64) for m in range(2)]
        evk = [keep.tile([P, RT, 4, P], BF16, name="evk%d" % g, align_bytes=64) for g in range(2)]
        evq0 = keep.tile([P, 4, N], BF16, name="evq0", align_bytes=64)
        evq1 = keep.tile([P, 2, 4, 256], BF16, name="evq1", align_bytes=64)
        osb = [keep.tile([P, N], F32, name="osb%d" % i) for i in range(RT)]
        warm = keep.tile([P, 512], BF16, name="warm")
        tiny = keep.tile([P, 1], F32, name="tiny")
        tiny2 = keep.tile([P, 1], F32, name="tiny2")

        words_in = [w_k_words, w_q_words]
        scales_in = [w_k_scales, w_q_scales]
        bias_in = [b_k, b_q]

        def load_scales(m):
            src = scales_in[m].bitcast(I32)
            dst = sst[m][:].bitcast(I32).rearrange("p (a c) -> p a c", a=2)
            for quad in range(4):
                nc.sync.dma_start(out=dst[32 * quad : 32 * quad + 4], in_=src[:, 4 * quad : 4 * quad + 4, :].rearrange("a q c -> q a c"))

        def load_words(m, g):
            src = words_in[m].bitcast(I32)
            dst = wst[m][g][:].bitcast(I32).rearrange("p (a c) -> p a c", a=2)
            nc.sync.dma_start(out=dst, in_=src[:, :, 256 * g : 256 * g + 256].rearrange("a p c -> p a c"))

        def load_bias(m):
            nc.sync.dma_start(
                out=brow[4 * m : 4 * m + 4, :].rearrange("s (q r) -> s q r", r=8),
                in_=bias_in[m].rearrange("(q s r) -> s q r", q=32, s=4),
            )

        def permute_words(m, g):
            src = wst[m][g][:].bitcast(I32).rearrange("p (a q s w) -> p a s q w", a=2, q=16, s=4)
            dst = wp[m][g][:].bitcast(I32).rearrange("p (a s q w) -> p a s q w", a=2, q=16, s=4)
            nc.vector.tensor_copy(out=dst, in_=src)

        def permute_scales(m, g):
            src = sst[m][:].bitcast(I32).rearrange("p (a g q s w) -> p g a s q w", a=2, g=2, q=16, s=4)
            dst = sp[m][g][:].bitcast(I32).rearrange("p (a s q w) -> p a s q w", a=2, q=16, s=4)
            nc.vector.tensor_copy(out=dst, in_=src[:, g])

        def transpose_h(i, g, b):
            words = hx[i][:].bitcast(F32)
            for u in range(2):
                c = (2 * g + u) * P
                nc.tensor.transpose(b[:, c : c + P], words[:, 256 * g + u : 256 * (g + 1) : 2], ident[:])

        def warm_up(n):
            for i in range(n):
                nc.tensor.matmul(dummy[:], warm[:, 0:P], warm[:], start=True, stop=True)

        def scale_h(i, g, b):
            t = work.tile([P, 4 * P], BF16, name="hgrp", align_bytes=64)
            src = b[:, 256 * g : 256 * g + 256].bitcast(BF16).rearrange("p (u n e) -> p n u e", u=2, e=2)
            dst = t[:].rearrange("p (n u e) -> p n u e", u=2, e=2)
            fac = hs[:, g, :].rearrange("p (u e) -> p u e", u=2).unsqueeze(1).to_broadcast([P, P, 2, 2])
            nc.vector.tensor_tensor(out=dst, in0=src, in1=fac, op=ALU.mult)
            return t

        def scale_h_planes(i, g, b):
            ph = work.tile([P, 4, P], BF16, name="hplane", align_bytes=64)
            src = b[:, 256 * g : 256 * g + 256].bitcast(BF16).rearrange("p (u n e) -> p u e n", u=2, e=2)
            for t in range(4):
                nc.scalar.activation(out=ph[:, t, :], in_=src[:, t // 2, t % 2], func=ACT.Copy, scale=hs[:, g, t : t + 1])
            return ph

        def weave_h(ph):
            t = work.tile([P, 4 * P], BF16, name="hgrp", align_bytes=64)
            nc.vector.tensor_copy(
                out=t[:].rearrange("p (c i s) -> p c s i", i=4, s=4),
                in_=ph[:].rearrange("p s (c i) -> p c s i", i=4),
            )
            return t

        def quant_h(i, g, t):
            cols = slice(P * i, P * i + P)
            nc.vector.quantize_mx(out=hq[:, g, cols].bitcast(FP8X4), scales=hqs[:, g, cols], in_=t[:])

        def project(m, g, s, cols, dst):
            for a in range(2):
                j = a * 4 + s
                nc.tensor.matmul_mx(
                    out=dst,
                    lhsT=wp[m][g][:, 256 * j : 256 * j + 256].bitcast(FP4X4),
                    lhsT_scale=sp[m][g][:, P * j : P * j + P],
                    rhs=hq[:, a, cols].bitcast(FP8X4),
                    rhs_scale=hqs[:, a, cols],
                    start=(a == 0),
                    stop=(a == 1),
                )

        def project_tile(m, g, i, b):
            for s in range(4):
                project(m, g, s, slice(P * i, P * i + P), b[:, P * s : P * s + P])

        def bias_col(m, g, s):
            j = g * 8 + m * 4 + s
            return bias[:, j : j + 1]

        def project_pair(m, g, h, s2, b):
            for i in range(2):
                for s in range(2):
                    c = 256 * s + P * i
                    project(m, g, 2 * s2 + s, slice(256 * h + P * i, 256 * h + P * i + P), b[:, c : c + P])

        def evac_pair(m, g, h, s2, b):
            for s in range(2):
                nc.scalar.activation(out=evq1[:, h, 2 * s2 + s, :], in_=b[:, 256 * s : 256 * s + 256], func=ACT.Identity, bias=bias_col(m, g, 2 * s2 + s))

        def fuse(m, g, i, b):
            t = work.tile([P, 4 * P], BF16, name="zgrp128", align_bytes=64)
            nc.vector.tensor_tensor(
                out=t[:].rearrange("p (n s) -> p n s", s=4),
                in0=b[:].rearrange("p (s n) -> p n s", s=4),
                in1=bias[:, 8 * g + 4 * m : 8 * g + 4 * m + 4].unsqueeze(1).to_broadcast([P, P, 4]),
                op=ALU.add,
            )
            return t

        def evac_s(m, g, s, b):
            nc.scalar.activation(out=evq0[:, s, :], in_=b[:], func=ACT.Identity, bias=bias_col(m, g, s))

        def evac_v(m, g, s, b):
            nc.vector.tensor_scalar(out=evq0[:, s, :], in0=b[:], scalar1=bias_col(m, g, s), scalar2=None, op0=ALU.add)

        def evac_tile(m, g, i, b):
            for s in range(4):
                nc.scalar.activation(out=evk[g][:, i, s, :], in_=b[:, P * s : P * s + P], func=ACT.Identity, bias=bias_col(m, g, s))

        def interleave(m, g, n0, n1):
            t = work.tile([P, 4 * (n1 - n0)], BF16, name="zgrp%d" % (n1 - n0), align_bytes=64)
            if m == 0:
                src = evk[g][:, n0 // P : n1 // P].rearrange("p b s (c i) -> p b c s i", i=4)
                dst = t[:].rearrange("p (b c i s) -> p b c s i", b=(n1 - n0) // P, i=4, s=4)
            else:
                h = n0 // 256
                rows = evq0[:, :, n0:n1] if g == 0 else evq1[:, h, :, n0 - 256 * h : n1 - 256 * h]
                src = rows.rearrange("p s (c i) -> p c s i", i=4)
                dst = t[:].rearrange("p (c i s) -> p c s i", i=4, s=4)
            nc.vector.tensor_copy(out=dst, in_=src)
            return t

        def quant_z(m, g, n0, n1, t):
            nc.vector.quantize_mx(out=zq[m][:, g, n0:n1].bitcast(FP8X4), scales=zqs[m][:, g, n0:n1], in_=t[:])

        def logits(i, b, g):
            rows = slice(P * i, P * i + P)
            nc.tensor.matmul_mx(
                out=b[:],
                lhsT=zq[1][:, g, rows].bitcast(FP8X4),
                lhsT_scale=zqs[1][:, g, rows],
                rhs=zq[0][:, g, :].bitcast(FP8X4),
                rhs_scale=zqs[0][:, g, :],
                start=(g == 0),
                stop=(g == 1),
            )

        dummy = bank(6)
        with tc.manual_schedule():
            nc.scalar.dma_start(out=hs[:], in_=h_scale.rearrange("o (g p t) -> p (o g) t", g=2, t=4))
            nc.vector.memset(tiny[:], 0.0)
            nc.scalar.activation(out=tiny2[:], in_=tiny[:], func=ACT.Identity)
            nc.vector.memset(sst[0][:].bitcast(I32), 0)
            nc.vector.memset(brow[:], 0.0)
            nc.gpsimd.memset(warm[:], 0.0)
            make_identity(nc, ident[:])
            nc.gpsimd.memset(sst[1][:].bitcast(I32), 0)
            hsrc = h_bytes.rearrange("(i p) k -> p i k", p=P)
            nc.sync.dma_start(out=hb[:, 0:1, :], in_=hsrc[:, 0:1, :])
            nc.sync.dma_start(out=hb[:, 1:2, :], in_=hsrc[:, 1:2, :])
            nc.sync.dma_start(out=hb[:, 2:4, :], in_=hsrc[:, 2:4, :])
            load_scales(0)
            load_words(0, 0)
            load_bias(0)
            load_bias(1)
            load_words(0, 1)
            load_scales(1)
            load_words(1, 0)
            load_words(1, 1)
            nc.vector.tensor_copy(out=ident16[:], in_=ident[:])

            warm_up(5)

            for half in range(2):
                cols = slice(512 * half, 512 * half + 512)
                nc.vector.tensor_copy(out=hx[0][:, cols], in_=hb[:, 0, cols].bitcast(FP8))
            nc.vector.tensor_copy(out=hx[1][:], in_=hb[:, 1, :].bitcast(FP8))
            for i in range(2, 4):
                nc.scalar.copy(out=hx[i][:], in_=hb[:, i, :].bitcast(FP8))
            tb = {}
            tb[0, 0] = bank(0)
            tb[0, 1] = bank(7)
            for i in range(1, 4):
                tb[i, 0] = tb[i, 1] = bank(i)
            for i in range(4):
                for g in range(2):
                    transpose_h(i, g, tb[i, g])
                warm_up([1, 2, 1, 0][i])
            ph20 = scale_h_planes(2, 0, tb[2, 0])
            ph21 = scale_h_planes(2, 1, tb[2, 1])


            t00 = scale_h(0, 0, tb[0, 0])
            kb = {}
            t01 = scale_h(0, 1, tb[0, 1])
            quant_h(0, 0, t00)
            permute_words(0, 0)
            permute_scales(0, 0)
            quant_h(0, 1, t01)
            kb[0, 0] = bank(4)
            project_tile(0, 0, 0, kb[0, 0])
            bb16 = bank(6)[:].bitcast(BF16)
            for g in range(2):
                nc.tensor.transpose(bb16[:, P * g : P * g + P], brow[:, P * g : P * g + P], ident16[:])
            nc.scalar.copy(out=bias[:].rearrange("p (g c) -> p g c", g=2), in_=bb16[:, 0:256].rearrange("p (g c) -> p g c", g=2)[:, :, 0:8])
            evac_tile(0, 0, 0, kb[0, 0])
            t10 = scale_h(1, 0, tb[1, 0])
            permute_words(0, 1)
            permute_scales(0, 1)
            kb[0, 1] = bank(5)
            project_tile(0, 1, 0, kb[0, 1])
            evac_tile(0, 1, 0, kb[0, 1])
            t11 = scale_h(1, 1, tb[1, 1])
            quant_h(1, 0, t10)
            t20 = weave_h(ph20)
            quant_h(1, 1, t11)
            kb[1, 0] = bank(6)
            project_tile(0, 0, 1, kb[1, 0])
            evac_tile(0, 0, 1, kb[1, 0])
            kb[1, 1] = bank(7)
            project_tile(0, 1, 1, kb[1, 1])
            evac_tile(0, 1, 1, kb[1, 1])
            t21 = weave_h(ph21)
            quant_h(2, 0, t20)
            t30 = scale_h(3, 0, tb[3, 0])
            quant_h(2, 1, t21)
            kb[2, 0] = bank(0)
            project_tile(0, 0, 2, kb[2, 0])
            evac_tile(0, 0, 2, kb[2, 0])
            kb[2, 1] = bank(1)
            project_tile(0, 1, 2, kb[2, 1])
            evac_tile(0, 1, 2, kb[2, 1])
            t31 = scale_h(3, 1, tb[3, 1])
            quant_h(3, 0, t30)
            permute_words(1, 0)
            quant_h(3, 1, t31)
            kb[3, 0] = bank(4)
            project_tile(0, 0, 3, kb[3, 0])
            evac_tile(0, 0, 3, kb[3, 0])
            permute_scales(1, 0)
            q0bank = [bank(2), bank(3), bank(6), bank(7)]
            for s in range(4):
                project(1, 0, s, slice(0, N), q0bank[s][:])
            evac_s(1, 0, 0, q0bank[0])
            evac_s(1, 0, 1, q0bank[1])
            evac_s(1, 0, 3, q0bank[3])
            ka = interleave(0, 0, 0, 256)
            kb1 = interleave(0, 1, 0, 256)
            quant_z(0, 0, 0, 256, ka)
            permute_words(1, 1)
            permute_scales(1, 1)
            kb[3, 1] = bank(5)
            project_tile(0, 1, 3, kb[3, 1])
            for h in range(2):
                for s2 in range(2):
                    b = bank([[0, 1], [4, 2]][h][s2])
                    project_pair(1, 1, h, s2, b)
                    evac_pair(1, 1, h, s2, b)
            ob = {}
            quant_z(0, 1, 0, 256, kb1)
            kd = interleave(0, 1, 256, 384)
            kc = interleave(0, 0, 256, 512)
            quant_z(0, 1, 256, 384, kd)
            evac_v(1, 0, 2, q0bank[2])
            quant_z(0, 0, 256, 512, kc)
            f31 = fuse(0, 1, 3, kb[3, 1])
            q0a = interleave(1, 0, 0, 256)
            quant_z(0, 1, 384, 512, f31)
            q0b = interleave(1, 0, 256, 512)
            quant_z(1, 0, 0, 256, q0a)
            for i in range(2):
                ob[i] = bank([3, 6, 7, 0][i])
                logits(i, ob[i], 0)
            q1a = interleave(1, 1, 0, 256)
            quant_z(1, 0, 256, 512, q0b)
            for i in range(2, RT):
                ob[i] = bank([3, 6, 7, 0][i])
                logits(i, ob[i], 0)
            quant_z(1, 1, 0, 256, q1a)
            q1b = interleave(1, 1, 256, 384)
            q1c = interleave(1, 1, 384, 512)
            quant_z(1, 1, 256, 384, q1b)
            quant_z(1, 1, 384, 512, q1c)
            for i in range(RT):
                logits(i, ob[i], 1)
                rows = slice(P * i, P * i + P)
                cut = [N // 2, N // 2, N // 2, N // 2][i]
                if cut:
                    nc.scalar.activation(out=osb[i][:, 0:cut], in_=ob[i][:, 0:cut], func=ACT.Copy, scale=SCALE)
                if cut < N:
                    nc.vector.tensor_scalar(out=osb[i][:, cut:N], in0=ob[i][:, cut:N], scalar1=SCALE, scalar2=None, op0=ALU.mult)
                nc.sync.dma_start(out=out[rows, :], in_=osb[i][:])
